import numpy as np
import ml_dtypes


def mxq(x, axis, fmt="e4m3"):
    dtype, down = {"e4m3": (ml_dtypes.float8_e4m3fn, 7), "e5m2": (ml_dtypes.float8_e5m2, 14)}[fmt]
    v = np.moveaxis(np.asarray(x, np.float32).astype(ml_dtypes.bfloat16).astype(np.float64), axis, -1)
    blocks = v.reshape(v.shape[:-1] + (-1, 32))
    amax = np.abs(blocks).max(-1, keepdims=True)
    byte = np.maximum(np.where(amax > 0, np.frexp(amax)[1] - 1 + 127, 0) - down, 1)
    scale = np.exp2(byte - 127.0)
    codes = (blocks / scale).astype(np.float32).astype(dtype).astype(np.float64)
    return np.moveaxis((codes * scale).reshape(v.shape), -1, axis)


WIDE = False


def mx_kscale(k):
    if not WIDE:
        return np.ones(k)
    levels = np.array([10, -10, 5, -5, 0])
    a = np.random.permutation(np.resize(levels, k // 512 * 4)).reshape(k // 512, 4)
    idx = np.arange(k)
    return np.exp2(a[idx // 512, idx % 128 // 32])


BF16 = ml_dtypes.bfloat16


def bf(x):
    return np.asarray(x, np.float32).astype(BF16)


def f64(x):
    return np.asarray(x).astype(np.float64)


E2M1 = np.array([0.0, 0.5, 1.0, 1.5, 2.0, 3.0, 4.0, 6.0, -0.0, -0.5, -1.0, -1.5, -2.0, -3.0, -4.0, -6.0])


def pack_weight(w, fmt):
    k, n = w.shape
    w = f64(bf(w)).reshape(k // 32, 32, n)
    amax = np.abs(w).max(1)
    if fmt == "e4m3":
        byte = np.frexp(amax)[1] - 1 + 127 - 7
    else:
        mant, ex = np.frexp(amax / 6.0)
        byte = np.where(mant > 0.5, ex, ex - 1) + 127
    byte = np.clip(np.where(amax > 0, byte, 1), 1, 254)
    scaled = (w * np.exp2(127.0 - byte)[:, None, :]).reshape(k, n).astype(np.float32)
    by_word = np.ascontiguousarray(scaled.reshape(k // 512, 128, 4, n).transpose(0, 1, 3, 2))
    if fmt == "e4m3":
        words = by_word.astype(ml_dtypes.float8_e4m3fn).view(np.uint8)
    else:
        c = by_word.astype(ml_dtypes.float4_e2m1fn).view(np.uint8) & 0xF
        words = c[..., 0::2] | (c[..., 1::2] << 4)
    return np.ascontiguousarray(words), np.ascontiguousarray(byte.astype(np.uint8).reshape(k // 512, 16, n))


def unpack_weight(words, scales, fmt):
    g, p, n, _ = words.shape
    if fmt == "e4m3":
        vals = np.ascontiguousarray(words).view(ml_dtypes.float8_e4m3fn).astype(np.float64)
    else:
        nib = np.empty((g, p, n, 4), np.uint8)
        nib[..., 0::2] = words & 0xF
        nib[..., 1::2] = words >> 4
        vals = E2M1[nib]
    vals = vals * np.repeat(np.exp2(scales.astype(np.float64) - 127.0), 8, axis=1)[..., None]
    return vals.transpose(0, 1, 3, 2).reshape(g * 512, n)


B, S, N, D = 2, 1, 128, 4096


def setup_inputs():
    s, t = mx_kscale(D), mx_kscale(D)
    tensor0 = bf(np.random.standard_normal((S, N, D)) * s)
    tensor1 = bf(np.random.standard_normal((S, N, D)) * 0.5 / t)
    kernel = np.random.standard_normal((D, D)) * D ** -0.75 * t[:, None] / s[None, :]
    words, scales = pack_weight(np.ascontiguousarray(kernel.T), "e4m3")
    bias = bf(0.5 + 0.1 * np.random.standard_normal(1))
    return {"tensor0": tensor0,
            "tensor1": tensor1,
            "kernel_words": words,
            "kernel_scales": scales,
            "bias": bias}


def reference(tensor0, tensor1, kernel_words, kernel_scales, bias):
    q = mxq(f64(tensor0), 2, "e4m3") @ unpack_weight(kernel_words, kernel_scales, "e4m3")
    out = mxq(f64(tensor1), 2, "e4m3") @ mxq(q, 2, "e4m3").transpose(0, 2, 1)
    out = out + f64(bias)
    return np.ascontiguousarray(np.broadcast_to(out[None], (B,) + out.shape))

@@ -1,0 +1,179 @@
+from contextlib import ExitStack
+
+import concourse.mybir as mybir
+from concourse.masks import make_identity
+
+F32 = mybir.dt.float32
+BF16 = mybir.dt.bfloat16
+I32 = mybir.dt.int32
+U32 = mybir.dt.uint32
+U8 = mybir.dt.uint8
+FP8X4 = mybir.dt.float8_e4m3fn_x4
+
+P = 128
+D = 4096
+K_PASS = 512
+NG = D // K_PASS
+
+FLOPS = 2 * P * D * D + 2 * P * P * D
+
+W_CHUNKS = ((0, 2048, 1), (2048, 1024, 2), (3072, 512, 4), (3584, 512, 4))
+
+
+def tile_bilinear_w_kernel(tc, tensor0, tensor1, kernel_words, kernel_scales, bias, out):
+    nc = tc.nc
+    with ExitStack() as ctx:
+        keep = ctx.enter_context(tc.tile_pool(name="keep", bufs=1))
+        work = ctx.enter_context(tc.tile_pool(name="work", bufs=3))
+        psum_tp = ctx.enter_context(tc.psum_pool(name="psum_tp", bufs=4))
+        psum_q = ctx.enter_context(tc.psum_pool(name="psum_q", bufs=3))
+        psum_acc = ctx.enter_context(tc.psum_pool(name="psum_acc", bufs=1))
+
+        wsc = keep.tile([P, 2, D], U8, align_bytes=64)
+        nc.vector.memset(wsc[:].rearrange("p h n -> p (h n)").bitcast(I32), 0)
+
+        ident32 = keep.tile([P, P], F32)
+        make_identity(nc, ident32[:])
+        identb = keep.tile([P, P], BF16)
+        make_identity(nc, identb[:])
+
+        bias_bf = keep.tile([P, 1], BF16)
+        nc.scalar.dma_start(out=bias_bf[:], in_=bias.partition_broadcast(P))
+
+        t0_sb = keep.tile([P, D], BF16)
+        nc.sync.dma_start(out=t0_sb[:], in_=tensor0[0, :, :])
+        t1_sb = keep.tile([P, D], BF16)
+        nc.sync.dma_start(out=t1_sb[:], in_=tensor1[0, :, :])
+
+        ks = kernel_scales.bitcast(I32)
+        for half in range(2):
+            for h in range(2):
+                for quad in (0, 2, 1, 3):
+                    nc.sync.dma_start(
+                        out=wsc[32 * quad : 32 * quad + 16, h, 2048 * half : 2048 * (half + 1)].bitcast(I32),
+                        in_=ks[4 * h : 4 * h + 4, 4 * quad : 4 * quad + 4, 512 * half : 512 * (half + 1)],
+                    )
+
+        kw = kernel_words.rearrange("g p n t -> g p (n t)").bitcast(I32)
+        w_at = {}
+        for c, (n0, cols, gper) in enumerate(W_CHUNKS):
+            for g0 in range(0, NG, gper):
+                wt = keep.tile([P, gper, cols], U32, name="w%d_%d" % (c, g0), align_bytes=64)
+                nc.sync.dma_start(
+                    out=wt[:].bitcast(I32),
+                    in_=kw[g0 : g0 + gper, :, n0 : n0 + cols].rearrange("g p n -> p g n"),
+                )
+                for gg in range(gper):
+                    w_at[(c, g0 + gg)] = (wt, gg)
+
+        bias32 = keep.tile([P, 1], F32)
+        nc.vector.tensor_copy(out=bias32[:], in_=bias_bf[:])
+
+        t0w = t0_sb[:].bitcast(F32)
+        t0g = keep.tile([P, NG, P, 4], BF16, align_bytes=64)
+        t0g32 = t0g[:].bitcast(F32)
+        t0c = keep.tile([P, NG, P], U32, align_bytes=64)
+        t0s = keep.tile([P, NG, P], U8, align_bytes=64)
+        for pair in range(NG // 2):
+            xt0 = psum_tp.tile([P, 2, 2, P], F32, tag="tp")
+            for gg in range(2):
+                g = 2 * pair + gg
+                for u in range(2):
+                    nc.tensor.transpose(
+                        out=xt0[:, gg, u, :],
+                        in_=t0w[:, 256 * g + u : 256 * (g + 1) : 2],
+                        identity=ident32[:],
+                    )
+            dst = t0g32[:, 2 * pair : 2 * pair + 2, :, :]
+            src = xt0[:].rearrange("p g u j -> p g j u")
+            if pair % 2 == 0:
+                nc.vector.tensor_copy(out=dst, in_=src)
+            else:
+                nc.scalar.copy(out=dst, in_=src)
+        for pair in range(NG // 2):
+            sl = slice(2 * pair, 2 * pair + 2)
+            nc.vector.quantize_mx(
+                out=t0c[:, sl, :].rearrange("p g j -> p (g j)").bitcast(FP8X4),
+                scales=t0s[:, sl, :].rearrange("p g j -> p (g j)"),
+                in_=t0g[:, sl, :, :].rearrange("p g j t -> p (g j t)"),
+            )
+
+        t1g = keep.tile([P, NG, P, 4], BF16, align_bytes=64)
+        t1c = keep.tile([P, NG, P], U32, align_bytes=64)
+        t1s = keep.tile([P, NG, P], U8, align_bytes=64)
+        for pair in range(NG // 2):
+            xt1 = psum_tp.tile([P, 2, 4, P], BF16, tag="tp")
+            for gg in range(2):
+                grp = 2 * pair + gg
+                for t in range(4):
+                    col = K_PASS * grp + P * t
+                    nc.tensor.transpose(out=xt1[:, gg, t, :], in_=t1_sb[:, col : col + P], identity=identb[:])
+            dst = t1g[:, 2 * pair : 2 * pair + 2, :, :]
+            src = xt1[:].rearrange("p g t i -> p g i t")
+            if pair % 2 == 0:
+                nc.scalar.copy(out=dst, in_=src)
+            else:
+                nc.vector.tensor_copy(out=dst, in_=src)
+        for pair in range(NG // 2):
+            sl = slice(2 * pair, 2 * pair + 2)
+            nc.vector.quantize_mx(
+                out=t1c[:, sl, :].rearrange("p g i -> p (g i)").bitcast(FP8X4),
+                scales=t1s[:, sl, :].rearrange("p g i -> p (g i)"),
+                in_=t1g[:, sl, :, :].rearrange("p g i t -> p (g i t)"),
+            )
+
+        qc = keep.tile([P, NG, P], U32, align_bytes=64)
+        qs = keep.tile([P, NG, P], U8, align_bytes=64)
+        acc = psum_acc.tile([P, P], F32)
+
+        def chunk_of(n):
+            for c, (n0, cols, gper) in enumerate(W_CHUNKS):
+                if n0 <= n < n0 + cols:
+                    return c, n - n0
+            raise ValueError("column outside W")
+
+        def first_stage(grp):
+            qps = psum_q.tile([P, 4, P], F32, tag="q")
+            for t in range(4):
+                n = K_PASS * grp + P * t
+                c, off = chunk_of(n)
+                for g in range(NG):
+                    wt, gg = w_at[(c, g)]
+                    nc.tensor.matmul_mx(
+                        out=qps[:, t, :],
+                        lhsT=wt[:, gg, off : off + P].bitcast(FP8X4),
+                        lhsT_scale=wsc[4 * (g % 4) : P, g // 4, n : n + P],
+                        rhs=t0c[:, g, :].bitcast(FP8X4),
+                        rhs_scale=t0s[:, g, :],
+                        start=(g == 0),
+                        stop=(g == NG - 1),
+                    )
+            qg = work.tile([P, P, 4], BF16, tag="qg", align_bytes=64)
+            nc.scalar.copy(out=qg[:], in_=qps[:].rearrange("p t j -> p j t"))
+            nc.vector.quantize_mx(
+                out=qc[:, grp, :].bitcast(FP8X4),
+                scales=qs[:, grp, :],
+                in_=qg[:].rearrange("p j t -> p (j t)"),
+            )
+
+        def second_stage(grp):
+            nc.tensor.matmul_mx(
+                out=acc[:],
+                lhsT=t1c[:, grp, :].bitcast(FP8X4),
+                lhsT_scale=t1s[:, grp, :],
+                rhs=qc[:, grp, :].bitcast(FP8X4),
+                rhs_scale=qs[:, grp, :],
+                start=(grp == 0),
+                stop=(grp == NG - 1),
+            )
+
+        first_stage(0)
+        for grp in range(1, NG):
+            first_stage(grp)
+            second_stage(grp - 1)
+        second_stage(NG - 1)
+
+        res = keep.tile([P, P], F32)
+        nc.vector.tensor_scalar_add(out=res[:], in0=acc[:], scalar1=bias32[:, 0:1])
+        nc.sync.dma_start(out=out[0, 0, :, :], in_=res[:])
+        nc.sync.dma_start(out=out[1, 0, :, :], in_=res[:])

@@ -17,7 +17,16 @@ NG = D // K_PASS
 
 FLOPS = 2 * P * D * D + 2 * P * P * D
 
-W_CHUNKS = ((0, 2048, 1), (2048, 1024, 2), (3072, 512, 4), (3584, 512, 4))
+
+def w_pieces():
+    whole = [(g, 0, D) for g in range(6)]
+    halves = [(6, 0, D // 2), (6, D // 2, D // 2)]
+    narrow = [(7, K_PASS * grp, K_PASS) for grp in range(NG)]
+    return whole + halves + narrow
+
+
+VECTOR_COPIES = (2, 5)
+LAG = 3
 
 
 def tile_bilinear_w_kernel(tc, tensor0, tensor1, kernel_words, kernel_scales, bias, out):
@@ -25,9 +34,8 @@ def tile_bilinear_w_kernel(tc, tensor0, tensor1, kernel_words, kernel_scales, bi
     with ExitStack() as ctx:
         keep = ctx.enter_context(tc.tile_pool(name="keep", bufs=1))
         work = ctx.enter_context(tc.tile_pool(name="work", bufs=3))
-        psum_tp = ctx.enter_context(tc.psum_pool(name="psum_tp", bufs=4))
-        psum_q = ctx.enter_context(tc.psum_pool(name="psum_q", bufs=3))
-        psum_acc = ctx.enter_context(tc.psum_pool(name="psum_acc", bufs=1))
+        psum = ctx.enter_context(tc.psum_pool(name="psum", bufs=8))
+        ctx.enter_context(tc.manual_schedule())
 
         wsc = keep.tile([P, 2, D], U8, align_bytes=64)
         nc.vector.memset(wsc[:].rearrange("p h n -> p (h n)").bitcast(I32), 0)
@@ -46,8 +54,8 @@ def tile_bilinear_w_kernel(tc, tensor0, tensor1, kernel_words, kernel_scales, bi
         nc.sync.dma_start(out=t1_sb[:], in_=tensor1[0, :, :])
 
         ks = kernel_scales.bitcast(I32)
-        for half in range(2):
-            for h in range(2):
+        for h in range(2):
+            for half in range(2):
                 for quad in (0, 2, 1, 3):
                     nc.sync.dma_start(
                         out=wsc[32 * quad : 32 * quad + 16, h, 2048 * half : 2048 * (half + 1)].bitcast(I32),
@@ -56,18 +64,11 @@ def tile_bilinear_w_kernel(tc, tensor0, tensor1, kernel_words, kernel_scales, bi
 
         kw = kernel_words.rearrange("g p n t -> g p (n t)").bitcast(I32)
         w_at = {}
-        for c, (n0, cols, gper) in enumerate(W_CHUNKS):
-            for g0 in range(0, NG, gper):
-                wt = keep.tile([P, gper, cols], U32, name="w%d_%d" % (c, g0), align_bytes=64)
-                nc.sync.dma_start(
-                    out=wt[:].bitcast(I32),
-                    in_=kw[g0 : g0 + gper, :, n0 : n0 + cols].rearrange("g p n -> p g n"),
-                )
-                for gg in range(gper):
-                    w_at[(c, g0 + gg)] = (wt, gg)
-
-        bias32 = keep.tile([P, 1], F32)
-        nc.vector.tensor_copy(out=bias32[:], in_=bias_bf[:])
+        for g, n0, cols in w_pieces():
+            wt = keep.tile([P, cols], U32, name="w%d_%d" % (g, n0), align_bytes=64)
+            nc.sync.dma_start(out=wt[:].bitcast(I32), in_=kw[g, :, n0 : n0 + cols])
+            for grp in range(n0 // K_PASS, (n0 + cols) // K_PASS):
+                w_at[(g, grp)] = (wt, K_PASS * grp - n0)
 
         t0w = t0_sb[:].bitcast(F32)
         t0g = keep.tile([P, NG, P, 4], BF16, align_bytes=64)
@@ -75,7 +76,7 @@ def tile_bilinear_w_kernel(tc, tensor0, tensor1, kernel_words, kernel_scales, bi
         t0c = keep.tile([P, NG, P], U32, align_bytes=64)
         t0s = keep.tile([P, NG, P], U8, align_bytes=64)
         for pair in range(NG // 2):
-            xt0 = psum_tp.tile([P, 2, 2, P], F32, tag="tp")
+            xt0 = psum.tile([P, 2, 2, P], F32, tag="bank")
             for gg in range(2):
                 g = 2 * pair + gg
                 for u in range(2):
@@ -90,8 +91,8 @@ def tile_bilinear_w_kernel(tc, tensor0, tensor1, kernel_words, kernel_scales, bi
                 nc.vector.tensor_copy(out=dst, in_=src)
             else:
                 nc.scalar.copy(out=dst, in_=src)
-        for pair in range(NG // 2):
-            sl = slice(2 * pair, 2 * pair + 2)
+        for half in range(2):
+            sl = slice(4 * half, 4 * half + 4)
             nc.vector.quantize_mx(
                 out=t0c[:, sl, :].rearrange("p g j -> p (g j)").bitcast(FP8X4),
                 scales=t0s[:, sl, :].rearrange("p g j -> p (g j)"),
@@ -102,7 +103,7 @@ def tile_bilinear_w_kernel(tc, tensor0, tensor1, kernel_words, kernel_scales, bi
         t1c = keep.tile([P, NG, P], U32, align_bytes=64)
         t1s = keep.tile([P, NG, P], U8, align_bytes=64)
         for pair in range(NG // 2):
-            xt1 = psum_tp.tile([P, 2, 4, P], BF16, tag="tp")
+            xt1 = psum.tile([P, 2, 4, P], BF16, tag="bank")
             for gg in range(2):
                 grp = 2 * pair + gg
                 for t in range(4):
@@ -114,51 +115,66 @@ def tile_bilinear_w_kernel(tc, tensor0, tensor1, kernel_words, kernel_scales, bi
                 nc.scalar.copy(out=dst, in_=src)
             else:
                 nc.vector.tensor_copy(out=dst, in_=src)
-        for pair in range(NG // 2):
-            sl = slice(2 * pair, 2 * pair + 2)
+        for half in range(2):
+            sl = slice(4 * half, 4 * half + 4)
             nc.vector.quantize_mx(
                 out=t1c[:, sl, :].rearrange("p g i -> p (g i)").bitcast(FP8X4),
                 scales=t1s[:, sl, :].rearrange("p g i -> p (g i)"),
                 in_=t1g[:, sl, :, :].rearrange("p g i t -> p (g i t)"),
             )
+        bias32 = keep.tile([P, 1], F32)
+        nc.vector.tensor_copy(out=bias32[:], in_=bias_bf[:])
 
         qc = keep.tile([P, NG, P], U32, align_bytes=64)
         qs = keep.tile([P, NG, P], U8, align_bytes=64)
-        acc = psum_acc.tile([P, P], F32)
+        qps = [psum.tile([P, 4, P], F32, tag="bank", name="qps%d" % grp) for grp in range(NG)]
 
-        def chunk_of(n):
-            for c, (n0, cols, gper) in enumerate(W_CHUNKS):
-                if n0 <= n < n0 + cols:
-                    return c, n - n0
-            raise ValueError("column outside W")
-
-        def first_stage(grp):
-            qps = psum_q.tile([P, 4, P], F32, tag="q")
+        def passes(g, grp):
+            wt, off = w_at[(g, grp)]
             for t in range(4):
                 n = K_PASS * grp + P * t
-                c, off = chunk_of(n)
-                for g in range(NG):
-                    wt, gg = w_at[(c, g)]
-                    nc.tensor.matmul_mx(
-                        out=qps[:, t, :],
-                        lhsT=wt[:, gg, off : off + P].bitcast(FP8X4),
-                        lhsT_scale=wsc[4 * (g % 4) : P, g // 4, n : n + P],
-                        rhs=t0c[:, g, :].bitcast(FP8X4),
-                        rhs_scale=t0s[:, g, :],
-                        start=(g == 0),
-                        stop=(g == NG - 1),
-                    )
+                nc.tensor.matmul_mx(
+                    out=qps[grp][:, t, :],
+                    lhsT=wt[:, off + P * t : off + P * (t + 1)].bitcast(FP8X4),
+                    lhsT_scale=wsc[4 * (g % 4) : P, g // 4, n : n + P],
+                    rhs=t0c[:, g, :].bitcast(FP8X4),
+                    rhs_scale=t0s[:, g, :],
+                    start=(g == 0 and t == 0),
+                    stop=(g == NG - 1 and t == 3),
+                )
+
+        for g in range(6):
+            for grp in range(NG):
+                passes(g, grp)
+        for grp in range(6):
+            passes(6, grp)
+
+        qgs = {}
+
+        def copy_out(grp):
             qg = work.tile([P, P, 4], BF16, tag="qg", align_bytes=64)
-            nc.scalar.copy(out=qg[:], in_=qps[:].rearrange("p t j -> p j t"))
+            qgs[grp] = qg
+            src = qps[grp][:].rearrange("p t j -> p j t")
+            if grp in VECTOR_COPIES:
+                nc.vector.tensor_copy(out=qg[:], in_=src)
+            else:
+                nc.scalar.copy(out=qg[:], in_=src)
+
+        def quantise(grp):
             nc.vector.quantize_mx(
                 out=qc[:, grp, :].bitcast(FP8X4),
                 scales=qs[:, grp, :],
-                in_=qg[:].rearrange("p j t -> p (j t)"),
+                in_=qgs[grp][:].rearrange("p j t -> p (j t)"),
             )
 
+        accs = []
+
         def second_stage(grp):
+            if grp == 0:
+                acc0 = psum.tile([P, P], F32, tag="bank")
+                accs.append(acc0)
             nc.tensor.matmul_mx(
-                out=acc[:],
+                out=accs[0][:],
                 lhsT=t1c[:, grp, :].bitcast(FP8X4),
                 lhsT_scale=t1s[:, grp, :],
                 rhs=qc[:, grp, :].bitcast(FP8X4),
@@ -167,13 +183,21 @@ def tile_bilinear_w_kernel(tc, tensor0, tensor1, kernel_words, kernel_scales, bi
                 stop=(grp == NG - 1),
             )
 
-        first_stage(0)
-        for grp in range(1, NG):
-            first_stage(grp)
-            second_stage(grp - 1)
-        second_stage(NG - 1)
+        for grp in range(NG):
+            passes(7, grp)
+            if grp + 6 < NG:
+                passes(6, grp + 6)
+            copy_out(grp)
+            if grp - 1 in VECTOR_COPIES:
+                quantise(grp - 1)
+            if grp not in VECTOR_COPIES:
+                quantise(grp)
+            if grp >= LAG:
+                second_stage(grp - LAG)
+        for grp in range(NG - LAG, NG):
+            second_stage(grp)
 
         res = keep.tile([P, P], F32)
-        nc.vector.tensor_scalar_add(out=res[:], in0=acc[:], scalar1=bias32[:, 0:1])
+        nc.vector.tensor_scalar_add(out=res[:], in0=accs[0][:], scalar1=bias32[:, 0:1])
         nc.sync.dma_start(out=out[0, 0, :, :], in_=res[:])
         nc.sync.dma_start(out=out[1, 0, :, :], in_=res[:])

@@ -55,12 +55,11 @@ def tile_bilinear_w_kernel(tc, tensor0, tensor1, kernel_words, kernel_scales, bi
 
         ks = kernel_scales.bitcast(I32)
         for h in range(2):
-            for half in range(2):
-                for quad in (0, 2, 1, 3):
-                    nc.sync.dma_start(
-                        out=wsc[32 * quad : 32 * quad + 16, h, 2048 * half : 2048 * (half + 1)].bitcast(I32),
-                        in_=ks[4 * h : 4 * h + 4, 4 * quad : 4 * quad + 4, 512 * half : 512 * (half + 1)],
-                    )
+            for quad in (0, 2, 1, 3):
+                nc.sync.dma_start(
+                    out=wsc[32 * quad : 32 * quad + 16, h, :].bitcast(I32),
+                    in_=ks[4 * h : 4 * h + 4, 4 * quad : 4 * quad + 4, :],
+                )
 
         kw = kernel_words.rearrange("g p n t -> g p (n t)").bitcast(I32)
         w_at = {}

@@ -37,16 +37,19 @@ def tile_bilinear_w_kernel(tc, tensor0, tensor1, kernel_words, kernel_scales, bi
         psum = ctx.enter_context(tc.psum_pool(name="psum", bufs=8))
         ctx.enter_context(tc.manual_schedule())
 
+        brow = keep.tile([P, 32], BF16)
+        nc.vector.memset(brow[:], 0.0)
         wsc = keep.tile([P, 2, D], U8, align_bytes=64)
         nc.vector.memset(wsc[:].rearrange("p h n -> p (h n)").bitcast(I32), 0)
+        ones = keep.tile([P, P], BF16)
+        nc.vector.memset(ones[:], 1.0)
 
         ident32 = keep.tile([P, P], F32)
         make_identity(nc, ident32[:])
         identb = keep.tile([P, P], BF16)
         make_identity(nc, identb[:])
 
-        bias_bf = keep.tile([P, 1], BF16)
-        nc.scalar.dma_start(out=bias_bf[:], in_=bias.partition_broadcast(P))
+        nc.scalar.dma_start(out=brow[0:1, 0:1], in_=bias.unsqueeze(0))
 
         t0_sb = keep.tile([P, D], BF16)
         nc.sync.dma_start(out=t0_sb[:], in_=tensor0[0, :, :])
@@ -55,11 +58,12 @@ def tile_bilinear_w_kernel(tc, tensor0, tensor1, kernel_words, kernel_scales, bi
 
         ks = kernel_scales.bitcast(I32)
         for h in range(2):
-            for quad in (0, 2, 1, 3):
-                nc.sync.dma_start(
-                    out=wsc[32 * quad : 32 * quad + 16, h, :].bitcast(I32),
-                    in_=ks[4 * h : 4 * h + 4, 4 * quad : 4 * quad + 4, :],
-                )
+            for half in range(2):
+                for quad in (0, 2, 1, 3):
+                    nc.sync.dma_start(
+                        out=wsc[32 * quad : 32 * quad + 16, h, 2048 * half : 2048 * (half + 1)].bitcast(I32),
+                        in_=ks[4 * h : 4 * h + 4, 4 * quad : 4 * quad + 4, 512 * half : 512 * (half + 1)],
+                    )
 
         kw = kernel_words.rearrange("g p n t -> g p (n t)").bitcast(I32)
         w_at = {}
@@ -68,6 +72,11 @@ def tile_bilinear_w_kernel(tc, tensor0, tensor1, kernel_words, kernel_scales, bi
             nc.sync.dma_start(out=wt[:].bitcast(I32), in_=kw[g, :, n0 : n0 + cols])
             for grp in range(n0 // K_PASS, (n0 + cols) // K_PASS):
                 w_at[(g, grp)] = (wt, K_PASS * grp - n0)
+
+        bps = psum.tile([P, 32], F32, tag="bank")
+        nc.tensor.matmul(out=bps[:], lhsT=ones[:], rhs=brow[:], start=True, stop=True)
+        bias32 = keep.tile([P, 1], F32)
+        nc.vector.tensor_copy(out=bias32[:], in_=bps[:, 0:1])
 
         t0w = t0_sb[:].bitcast(F32)
         t0g = keep.tile([P, NG, P, 4], BF16, align_bytes=64)
@@ -121,8 +130,6 @@ def tile_bilinear_w_kernel(tc, tensor0, tensor1, kernel_words, kernel_scales, bi
                 scales=t1s[:, sl, :].rearrange("p g i -> p (g i)"),
                 in_=t1g[:, sl, :, :].rearrange("p g i t -> p (g i t)"),
             )
-        bias32 = keep.tile([P, 1], F32)
-        nc.vector.tensor_copy(out=bias32[:], in_=bias_bf[:])
 
         qc = keep.tile([P, NG, P], U32, align_bytes=64)
         qs = keep.tile([P, NG, P], U8, align_bytes=64)

@@ -21,19 +21,19 @@ FLOPS = 2 * P * D * D + 2 * P * P * D
 def w_pieces():
     whole = [(g, 0, D) for g in range(6)]
     halves = [(6, 0, D // 2), (6, D // 2, D // 2)]
-    narrow = [(7, K_PASS * grp, K_PASS) for grp in range(NG)]
+    narrow = [(7, 0, 1024), (7, 1024, 1024), (7, 2048, 1024), (7, 3072, 512), (7, 3584, 512)]
     return whole + halves + narrow
 
 
-VECTOR_COPIES = (2, 5)
-LAG = 3
+VECTOR_COPIES = (1, 3, 5)
+LAG = 4
 
 
 def tile_bilinear_w_kernel(tc, tensor0, tensor1, kernel_words, kernel_scales, bias, out):
     nc = tc.nc
     with ExitStack() as ctx:
         keep = ctx.enter_context(tc.tile_pool(name="keep", bufs=1))
-        work = ctx.enter_context(tc.tile_pool(name="work", bufs=3))
+        work = ctx.enter_context(tc.tile_pool(name="work", bufs=4))
         psum = ctx.enter_context(tc.psum_pool(name="psum", bufs=8))
         ctx.enter_context(tc.manual_schedule())
 
@@ -149,11 +149,9 @@ def tile_bilinear_w_kernel(tc, tensor0, tensor1, kernel_words, kernel_scales, bi
                     stop=(g == NG - 1 and t == 3),
                 )
 
-        for g in range(6):
+        for g in range(7):
             for grp in range(NG):
                 passes(g, grp)
-        for grp in range(6):
-            passes(6, grp)
 
         qgs = {}
 
@@ -191,12 +189,11 @@ def tile_bilinear_w_kernel(tc, tensor0, tensor1, kernel_words, kernel_scales, bi
 
         for grp in range(NG):
             passes(7, grp)
-            if grp + 6 < NG:
-                passes(6, grp + 6)
             copy_out(grp)
-            if grp - 1 in VECTOR_COPIES:
+            if grp in VECTOR_COPIES:
                 quantise(grp - 1)
-            if grp not in VECTOR_COPIES:
+                quantise(grp)
+            elif grp + 1 not in VECTOR_COPIES:
                 quantise(grp)
             if grp >= LAG:
                 second_stage(grp - LAG)

@@ -11,58 +11,61 @@ U8 = mybir.dt.uint8
 FP8X4 = mybir.dt.float8_e4m3fn_x4
 
 P = 128
+PACK = 4
 D = 4096
-K_PASS = 512
-NG = D // K_PASS
+K_PASS = P * PACK
+GROUPS = D // K_PASS
+BANKS = D // K_PASS
+LAST = GROUPS - 1
 
 FLOPS = 2 * P * D * D + 2 * P * P * D
 
+PLANES = 4
+EARLY_BANKS = 6
+VECTOR_COPIES = (2, 5)
+LAG = 3
+BIAS_COLS = 32
+
 
 def w_pieces():
-    whole = [(g, 0, D) for g in range(6)]
-    halves = [(6, 0, D // 2), (6, D // 2, D // 2)]
-    narrow = [(7, 0, 1024), (7, 1024, 1024), (7, 2048, 1024), (7, 3072, 512), (7, 3584, 512)]
+    whole = [(g, 0, D) for g in range(LAST - 1)]
+    halves = [(LAST - 1, 0, D // 2), (LAST - 1, D // 2, D // 2)]
+    narrow = [(LAST, K_PASS * bank, K_PASS) for bank in range(BANKS)]
     return whole + halves + narrow
-
-
-VECTOR_COPIES = (1, 3, 5)
-LAG = 4
 
 
 def tile_bilinear_w_kernel(tc, tensor0, tensor1, kernel_words, kernel_scales, bias, out):
     nc = tc.nc
     with ExitStack() as ctx:
         keep = ctx.enter_context(tc.tile_pool(name="keep", bufs=1))
-        work = ctx.enter_context(tc.tile_pool(name="work", bufs=4))
+        work = ctx.enter_context(tc.tile_pool(name="work", bufs=3))
         psum = ctx.enter_context(tc.psum_pool(name="psum", bufs=8))
         ctx.enter_context(tc.manual_schedule())
 
-        brow = keep.tile([P, 32], BF16)
+        brow = keep.tile([P, BIAS_COLS], BF16)
         nc.vector.memset(brow[:], 0.0)
-        wsc = keep.tile([P, 2, D], U8, align_bytes=64)
+        wsc = keep.tile([P, GROUPS // PLANES, D], U8, align_bytes=64)
         nc.vector.memset(wsc[:].rearrange("p h n -> p (h n)").bitcast(I32), 0)
         ones = keep.tile([P, P], BF16)
         nc.vector.memset(ones[:], 1.0)
-
         ident32 = keep.tile([P, P], F32)
         make_identity(nc, ident32[:])
         identb = keep.tile([P, P], BF16)
         make_identity(nc, identb[:])
 
-        nc.scalar.dma_start(out=brow[0:1, 0:1], in_=bias.unsqueeze(0))
-
         t0_sb = keep.tile([P, D], BF16)
         nc.sync.dma_start(out=t0_sb[:], in_=tensor0[0, :, :])
         t1_sb = keep.tile([P, D], BF16)
         nc.sync.dma_start(out=t1_sb[:], in_=tensor1[0, :, :])
+        nc.sync.dma_start(out=brow[0:1, 0:1], in_=bias.unsqueeze(0))
 
         ks = kernel_scales.bitcast(I32)
-        for h in range(2):
+        for h in range(GROUPS // PLANES):
             for half in range(2):
                 for quad in (0, 2, 1, 3):
                     nc.sync.dma_start(
                         out=wsc[32 * quad : 32 * quad + 16, h, 2048 * half : 2048 * (half + 1)].bitcast(I32),
-                        in_=ks[4 * h : 4 * h + 4, 4 * quad : 4 * quad + 4, 512 * half : 512 * (half + 1)],
+                        in_=ks[PLANES * h : PLANES * (h + 1), 4 * quad : 4 * quad + 4, 512 * half : 512 * (half + 1)],
                     )
 
         kw = kernel_words.rearrange("g p n t -> g p (n t)").bitcast(I32)
@@ -70,20 +73,15 @@ def tile_bilinear_w_kernel(tc, tensor0, tensor1, kernel_words, kernel_scales, bi
         for g, n0, cols in w_pieces():
             wt = keep.tile([P, cols], U32, name="w%d_%d" % (g, n0), align_bytes=64)
             nc.sync.dma_start(out=wt[:].bitcast(I32), in_=kw[g, :, n0 : n0 + cols])
-            for grp in range(n0 // K_PASS, (n0 + cols) // K_PASS):
-                w_at[(g, grp)] = (wt, K_PASS * grp - n0)
-
-        bps = psum.tile([P, 32], F32, tag="bank")
-        nc.tensor.matmul(out=bps[:], lhsT=ones[:], rhs=brow[:], start=True, stop=True)
-        bias32 = keep.tile([P, 1], F32)
-        nc.vector.tensor_copy(out=bias32[:], in_=bps[:, 0:1])
+            for bank in range(n0 // K_PASS, (n0 + cols) // K_PASS):
+                w_at[(g, bank)] = (wt, K_PASS * bank - n0)
 
         t0w = t0_sb[:].bitcast(F32)
-        t0g = keep.tile([P, NG, P, 4], BF16, align_bytes=64)
+        t0g = keep.tile([P, GROUPS, P, PACK], BF16, align_bytes=64)
         t0g32 = t0g[:].bitcast(F32)
-        t0c = keep.tile([P, NG, P], U32, align_bytes=64)
-        t0s = keep.tile([P, NG, P], U8, align_bytes=64)
-        for pair in range(NG // 2):
+        t0c = keep.tile([P, GROUPS, P], U32, align_bytes=64)
+        t0s = keep.tile([P, GROUPS, P], U8, align_bytes=64)
+        for pair in range(GROUPS // 2):
             xt0 = psum.tile([P, 2, 2, P], F32, tag="bank")
             for gg in range(2):
                 g = 2 * pair + gg
@@ -100,107 +98,105 @@ def tile_bilinear_w_kernel(tc, tensor0, tensor1, kernel_words, kernel_scales, bi
             else:
                 nc.scalar.copy(out=dst, in_=src)
         for half in range(2):
-            sl = slice(4 * half, 4 * half + 4)
+            sl = slice(GROUPS // 2 * half, GROUPS // 2 * (half + 1))
             nc.vector.quantize_mx(
                 out=t0c[:, sl, :].rearrange("p g j -> p (g j)").bitcast(FP8X4),
                 scales=t0s[:, sl, :].rearrange("p g j -> p (g j)"),
                 in_=t0g[:, sl, :, :].rearrange("p g j t -> p (g j t)"),
             )
 
-        t1g = keep.tile([P, NG, P, 4], BF16, align_bytes=64)
-        t1c = keep.tile([P, NG, P], U32, align_bytes=64)
-        t1s = keep.tile([P, NG, P], U8, align_bytes=64)
-        for pair in range(NG // 2):
-            xt1 = psum.tile([P, 2, 4, P], BF16, tag="bank")
-            for gg in range(2):
-                grp = 2 * pair + gg
-                for t in range(4):
-                    col = K_PASS * grp + P * t
-                    nc.tensor.transpose(out=xt1[:, gg, t, :], in_=t1_sb[:, col : col + P], identity=identb[:])
+        t1g = keep.tile([P, BANKS, P, PACK], BF16, align_bytes=64)
+        t1c = keep.tile([P, BANKS, P], U32, align_bytes=64)
+        t1s = keep.tile([P, BANKS, P], U8, align_bytes=64)
+        for pair in range(BANKS // 2):
+            xt1 = psum.tile([P, 2, PACK, P], BF16, tag="bank")
+            for bb in range(2):
+                bank = 2 * pair + bb
+                for t in range(PACK):
+                    col = K_PASS * bank + P * t
+                    nc.tensor.transpose(out=xt1[:, bb, t, :], in_=t1_sb[:, col : col + P], identity=identb[:])
             dst = t1g[:, 2 * pair : 2 * pair + 2, :, :]
-            src = xt1[:].rearrange("p g t i -> p g i t")
+            src = xt1[:].rearrange("p b t i -> p b i t")
             if pair % 2 == 0:
                 nc.scalar.copy(out=dst, in_=src)
             else:
                 nc.vector.tensor_copy(out=dst, in_=src)
         for half in range(2):
-            sl = slice(4 * half, 4 * half + 4)
+            sl = slice(BANKS // 2 * half, BANKS // 2 * (half + 1))
             nc.vector.quantize_mx(
-                out=t1c[:, sl, :].rearrange("p g i -> p (g i)").bitcast(FP8X4),
-                scales=t1s[:, sl, :].rearrange("p g i -> p (g i)"),
-                in_=t1g[:, sl, :, :].rearrange("p g i t -> p (g i t)"),
+                out=t1c[:, sl, :].rearrange("p b i -> p (b i)").bitcast(FP8X4),
+                scales=t1s[:, sl, :].rearrange("p b i -> p (b i)"),
+                in_=t1g[:, sl, :, :].rearrange("p b i t -> p (b i t)"),
             )
 
-        qc = keep.tile([P, NG, P], U32, align_bytes=64)
-        qs = keep.tile([P, NG, P], U8, align_bytes=64)
-        qps = [psum.tile([P, 4, P], F32, tag="bank", name="qps%d" % grp) for grp in range(NG)]
+        bps = psum.tile([P, BIAS_COLS], F32, tag="bank")
+        nc.tensor.matmul(out=bps[:], lhsT=ones[:], rhs=brow[:], start=True, stop=True)
+        bias32 = keep.tile([P, 1], F32)
+        nc.vector.tensor_copy(out=bias32[:], in_=bps[:, 0:1])
 
-        def passes(g, grp):
-            wt, off = w_at[(g, grp)]
-            for t in range(4):
-                n = K_PASS * grp + P * t
+        qc = keep.tile([P, BANKS, P], U32, align_bytes=64)
+        qs = keep.tile([P, BANKS, P], U8, align_bytes=64)
+        qps = [psum.tile([P, PACK, P], F32, tag="bank", name="qps%d" % bank) for bank in range(BANKS)]
+
+        def first_product(g, bank):
+            wt, off = w_at[(g, bank)]
+            for t in range(PACK):
+                n = K_PASS * bank + P * t
                 nc.tensor.matmul_mx(
-                    out=qps[grp][:, t, :],
+                    out=qps[bank][:, t, :],
                     lhsT=wt[:, off + P * t : off + P * (t + 1)].bitcast(FP8X4),
-                    lhsT_scale=wsc[4 * (g % 4) : P, g // 4, n : n + P],
+                    lhsT_scale=wsc[4 * (g % PLANES) : P, g // PLANES, n : n + P],
                     rhs=t0c[:, g, :].bitcast(FP8X4),
                     rhs_scale=t0s[:, g, :],
                     start=(g == 0 and t == 0),
-                    stop=(g == NG - 1 and t == 3),
+                    stop=(g == LAST and t == PACK - 1),
                 )
 
-        for g in range(7):
-            for grp in range(NG):
-                passes(g, grp)
-
-        qgs = {}
-
-        def copy_out(grp):
-            qg = work.tile([P, P, 4], BF16, tag="qg", align_bytes=64)
-            qgs[grp] = qg
-            src = qps[grp][:].rearrange("p t j -> p j t")
-            if grp in VECTOR_COPIES:
+        def quantise_q(bank):
+            qg = work.tile([P, P, PACK], BF16, tag="qg", align_bytes=64)
+            src = qps[bank][:].rearrange("p t j -> p j t")
+            if bank in VECTOR_COPIES:
                 nc.vector.tensor_copy(out=qg[:], in_=src)
             else:
                 nc.scalar.copy(out=qg[:], in_=src)
-
-        def quantise(grp):
             nc.vector.quantize_mx(
-                out=qc[:, grp, :].bitcast(FP8X4),
-                scales=qs[:, grp, :],
-                in_=qgs[grp][:].rearrange("p j t -> p (j t)"),
+                out=qc[:, bank, :].bitcast(FP8X4),
+                scales=qs[:, bank, :],
+                in_=qg[:].rearrange("p j t -> p (j t)"),
             )
 
-        accs = []
-
-        def second_stage(grp):
-            if grp == 0:
-                acc0 = psum.tile([P, P], F32, tag="bank")
-                accs.append(acc0)
+        def second_product(acc, bank):
             nc.tensor.matmul_mx(
-                out=accs[0][:],
-                lhsT=t1c[:, grp, :].bitcast(FP8X4),
-                lhsT_scale=t1s[:, grp, :],
-                rhs=qc[:, grp, :].bitcast(FP8X4),
-                rhs_scale=qs[:, grp, :],
-                start=(grp == 0),
-                stop=(grp == NG - 1),
+                out=acc[:],
+                lhsT=t1c[:, bank, :].bitcast(FP8X4),
+                lhsT_scale=t1s[:, bank, :],
+                rhs=qc[:, bank, :].bitcast(FP8X4),
+                rhs_scale=qs[:, bank, :],
+                start=(bank == 0),
+                stop=(bank == BANKS - 1),
             )
 
-        for grp in range(NG):
-            passes(7, grp)
-            copy_out(grp)
-            if grp in VECTOR_COPIES:
-                quantise(grp - 1)
-                quantise(grp)
-            elif grp + 1 not in VECTOR_COPIES:
-                quantise(grp)
-            if grp >= LAG:
-                second_stage(grp - LAG)
-        for grp in range(NG - LAG, NG):
-            second_stage(grp)
+        def close(bank):
+            first_product(LAST, bank)
+            if bank + EARLY_BANKS < BANKS:
+                first_product(LAST - 1, bank + EARLY_BANKS)
+            quantise_q(bank)
+
+        for g in range(LAST - 1):
+            for bank in range(BANKS):
+                first_product(g, bank)
+        for bank in range(EARLY_BANKS):
+            first_product(LAST - 1, bank)
+        for bank in range(LAG):
+            close(bank)
+        acc = psum.tile([P, P], F32, tag="bank")
+        for bank in range(LAG, BANKS):
+            close(bank)
+            second_product(acc, bank - LAG)
+        for bank in range(BANKS - LAG, BANKS):
+            second_product(acc, bank)
 
         res = keep.tile([P, P], F32)
-        nc.vector.tensor_scalar_add(out=res[:], in0=accs[0][:], scalar1=bias32[:, 0:1])
+        nc.vector.tensor_scalar_add(out=res[:], in0=acc[:], scalar1=bias32[:, 0:1])
         nc.sync.dma_start(out=out[0, 0, :, :], in_=res[:])
         nc.sync.dma_start(out=out[1, 0, :, :], in_=res[:])

from contextlib import ExitStack

import concourse.mybir as mybir
from concourse.masks import make_identity

F32 = mybir.dt.float32
BF16 = mybir.dt.bfloat16
I32 = mybir.dt.int32
U32 = mybir.dt.uint32
U8 = mybir.dt.uint8
FP8X4 = mybir.dt.float8_e4m3fn_x4

P = 128
PACK = 4
D = 4096
K_PASS = P * PACK
GROUPS = D // K_PASS
BANKS = D // K_PASS
LAST = GROUPS - 1

FLOPS = 2 * P * D * D + 2 * P * P * D

PLANES = 4
EARLY_BANKS = 6
VECTOR_COPIES = (2, 5)
LAG = 3
BIAS_COLS = 32


def w_pieces():
    whole = [(g, 0, D) for g in range(LAST - 1)]
    halves = [(LAST - 1, 0, D // 2), (LAST - 1, D // 2, D // 2)]
    narrow = [(LAST, K_PASS * bank, K_PASS) for bank in range(BANKS)]
    return whole + halves + narrow


def tile_bilinear_w_kernel(tc, tensor0, tensor1, kernel_words, kernel_scales, bias, out):
    nc = tc.nc
    with ExitStack() as ctx:
        keep = ctx.enter_context(tc.tile_pool(name="keep", bufs=1))
        work = ctx.enter_context(tc.tile_pool(name="work", bufs=3))
        psum = ctx.enter_context(tc.psum_pool(name="psum", bufs=8))
        ctx.enter_context(tc.manual_schedule())

        brow = keep.tile([P, BIAS_COLS], BF16)
        nc.vector.memset(brow[:], 0.0)
        wsc = keep.tile([P, GROUPS // PLANES, D], U8, align_bytes=64)
        nc.vector.memset(wsc[:].rearrange("p h n -> p (h n)").bitcast(I32), 0)
        ones = keep.tile([P, P], BF16)
        nc.vector.memset(ones[:], 1.0)
        ident32 = keep.tile([P, P], F32)
        make_identity(nc, ident32[:])
        identb = keep.tile([P, P], BF16)
        make_identity(nc, identb[:])

        t0_sb = keep.tile([P, D], BF16)
        nc.sync.dma_start(out=t0_sb[:], in_=tensor0[0, :, :])
        t1_sb = keep.tile([P, D], BF16)
        nc.sync.dma_start(out=t1_sb[:], in_=tensor1[0, :, :])
        nc.sync.dma_start(out=brow[0:1, 0:1], in_=bias.unsqueeze(0))

        ks = kernel_scales.bitcast(I32)
        for h in range(GROUPS // PLANES):
            for half in range(2):
                for quad in (0, 2, 1, 3):
                    nc.sync.dma_start(
                        out=wsc[32 * quad : 32 * quad + 16, h, 2048 * half : 2048 * (half + 1)].bitcast(I32),
                        in_=ks[PLANES * h : PLANES * (h + 1), 4 * quad : 4 * quad + 4, 512 * half : 512 * (half + 1)],
                    )

        kw = kernel_words.rearrange("g p n t -> g p (n t)").bitcast(I32)
        w_at = {}
        for g, n0, cols in w_pieces():
            wt = keep.tile([P, cols], U32, name="w%d_%d" % (g, n0), align_bytes=64)
            nc.sync.dma_start(out=wt[:].bitcast(I32), in_=kw[g, :, n0 : n0 + cols])
            for bank in range(n0 // K_PASS, (n0 + cols) // K_PASS):
                w_at[(g, bank)] = (wt, K_PASS * bank - n0)

        t0w = t0_sb[:].bitcast(F32)
        t0g = keep.tile([P, GROUPS, P, PACK], BF16, align_bytes=64)
        t0g32 = t0g[:].bitcast(F32)
        t0c = keep.tile([P, GROUPS, P], U32, align_bytes=64)
        t0s = keep.tile([P, GROUPS, P], U8, align_bytes=64)
        for pair in range(GROUPS // 2):
            xt0 = psum.tile([P, 2, 2, P], F32, tag="bank")
            for gg in range(2):
                g = 2 * pair + gg
                for u in range(2):
                    nc.tensor.transpose(
                        out=xt0[:, gg, u, :],
                        in_=t0w[:, 256 * g + u : 256 * (g + 1) : 2],
                        identity=ident32[:],
                    )
            dst = t0g32[:, 2 * pair : 2 * pair + 2, :, :]
            src = xt0[:].rearrange("p g u j -> p g j u")
            if pair % 2 == 0:
                nc.vector.tensor_copy(out=dst, in_=src)
            else:
                nc.scalar.copy(out=dst, in_=src)
        for half in range(2):
            sl = slice(GROUPS // 2 * half, GROUPS // 2 * (half + 1))
            nc.vector.quantize_mx(
                out=t0c[:, sl, :].rearrange("p g j -> p (g j)").bitcast(FP8X4),
                scales=t0s[:, sl, :].rearrange("p g j -> p (g j)"),
                in_=t0g[:, sl, :, :].rearrange("p g j t -> p (g j t)"),
            )

        t1g = keep.tile([P, BANKS, P, PACK], BF16, align_bytes=64)
        t1c = keep.tile([P, BANKS, P], U32, align_bytes=64)
        t1s = keep.tile([P, BANKS, P], U8, align_bytes=64)
        for pair in range(BANKS // 2):
            xt1 = psum.tile([P, 2, PACK, P], BF16, tag="bank")
            for bb in range(2):
                bank = 2 * pair + bb
                for t in range(PACK):
                    col = K_PASS * bank + P * t
                    nc.tensor.transpose(out=xt1[:, bb, t, :], in_=t1_sb[:, col : col + P], identity=identb[:])
            dst = t1g[:, 2 * pair : 2 * pair + 2, :, :]
            src = xt1[:].rearrange("p b t i -> p b i t")
            if pair % 2 == 0:
                nc.scalar.copy(out=dst, in_=src)
            else:
                nc.vector.tensor_copy(out=dst, in_=src)
        for half in range(2):
            sl = slice(BANKS // 2 * half, BANKS // 2 * (half + 1))
            nc.vector.quantize_mx(
                out=t1c[:, sl, :].rearrange("p b i -> p (b i)").bitcast(FP8X4),
                scales=t1s[:, sl, :].rearrange("p b i -> p (b i)"),
                in_=t1g[:, sl, :, :].rearrange("p b i t -> p (b i t)"),
            )

        bps = psum.tile([P, BIAS_COLS], F32, tag="bank")
        nc.tensor.matmul(out=bps[:], lhsT=ones[:], rhs=brow[:], start=True, stop=True)
        bias32 = keep.tile([P, 1], F32)
        nc.vector.tensor_copy(out=bias32[:], in_=bps[:, 0:1])

        qc = keep.tile([P, BANKS, P], U32, align_bytes=64)
        qs = keep.tile([P, BANKS, P], U8, align_bytes=64)
        qps = [psum.tile([P, PACK, P], F32, tag="bank", name="qps%d" % bank) for bank in range(BANKS)]

        def first_product(g, bank):
            wt, off = w_at[(g, bank)]
            for t in range(PACK):
                n = K_PASS * bank + P * t
                nc.tensor.matmul_mx(
                    out=qps[bank][:, t, :],
                    lhsT=wt[:, off + P * t : off + P * (t + 1)].bitcast(FP8X4),
                    lhsT_scale=wsc[4 * (g % PLANES) : P, g // PLANES, n : n + P],
                    rhs=t0c[:, g, :].bitcast(FP8X4),
                    rhs_scale=t0s[:, g, :],
                    start=(g == 0 and t == 0),
                    stop=(g == LAST and t == PACK - 1),
                )

        def quantise_q(bank):
            qg = work.tile([P, P, PACK], BF16, tag="qg", align_bytes=64)
            src = qps[bank][:].rearrange("p t j -> p j t")
            if bank in VECTOR_COPIES:
                nc.vector.tensor_copy(out=qg[:], in_=src)
            else:
                nc.scalar.copy(out=qg[:], in_=src)
            nc.vector.quantize_mx(
                out=qc[:, bank, :].bitcast(FP8X4),
                scales=qs[:, bank, :],
                in_=qg[:].rearrange("p j t -> p (j t)"),
            )

        def second_product(acc, bank):
            nc.tensor.matmul_mx(
                out=acc[:],
                lhsT=t1c[:, bank, :].bitcast(FP8X4),
                lhsT_scale=t1s[:, bank, :],
                rhs=qc[:, bank, :].bitcast(FP8X4),
                rhs_scale=qs[:, bank, :],
                start=(bank == 0),
                stop=(bank == BANKS - 1),
            )

        def close(bank):
            first_product(LAST, bank)
            if bank + EARLY_BANKS < BANKS:
                first_product(LAST - 1, bank + EARLY_BANKS)
            quantise_q(bank)

        for g in range(LAST - 1):
            for bank in range(BANKS):
                first_product(g, bank)
        for bank in range(EARLY_BANKS):
            first_product(LAST - 1, bank)
        for bank in range(LAG):
            close(bank)
        acc = psum.tile([P, P], F32, tag="bank")
        for bank in range(LAG, BANKS):
            close(bank)
            second_product(acc, bank - LAG)
        for bank in range(BANKS - LAG, BANKS):
            second_product(acc, bank)

        res = keep.tile([P, P], F32)
        nc.vector.tensor_scalar_add(out=res[:], in0=acc[:], scalar1=bias32[:, 0:1])
        nc.sync.dma_start(out=out[0, 0, :, :], in_=res[:])
        nc.sync.dma_start(out=out[1, 0, :, :], in_=res[:])
